import numpy as np
import ml_dtypes


def mxq(x, axis, fmt="e4m3"):
    dtype, down = {"e4m3": (ml_dtypes.float8_e4m3fn, 7), "e5m2": (ml_dtypes.float8_e5m2, 14)}[fmt]
    v = np.moveaxis(np.asarray(x, np.float32).astype(ml_dtypes.bfloat16).astype(np.float64), axis, -1)
    blocks = v.reshape(v.shape[:-1] + (-1, 32))
    amax = np.abs(blocks).max(-1, keepdims=True)
    byte = np.maximum(np.where(amax > 0, np.frexp(amax)[1] - 1 + 127, 0) - down, 1)
    scale = np.exp2(byte - 127.0)
    codes = (blocks / scale).astype(np.float32).astype(dtype).astype(np.float64)
    return np.moveaxis((codes * scale).reshape(v.shape), -1, axis)


WIDE = False


def mx_kscale(k):
    if not WIDE:
        return np.ones(k)
    levels = np.array([10, -10, 5, -5, 0])
    if k % 512:
        return np.exp2(np.random.permutation(np.resize(levels, k // 32))).repeat(32)
    a = np.empty((k // 512, 16))
    for p in range(k // 512):
        a[p, :8] = np.random.permutation(np.resize(levels, 8))
        for g in range(8):
            far = levels[np.abs(levels - a[p, g]) >= 10]
            a[p, g + 8] = far[np.random.randint(len(far))]
    return np.exp2(a.ravel()).repeat(32)


BF16 = ml_dtypes.bfloat16


def bf(x):
    return np.asarray(x, np.float32).astype(BF16)


def f64(x):
    return np.asarray(x).astype(np.float64)


B, GF, GH, GW, DM, NH, HD, L = 1, 4, 8, 16, 2048, 16, 128, 1024
S = GF * GH * GW
DI = NH * HD
C = HD // 2
EPS = 1e-6


def rms(t, g):
    return t * (1.0 / np.sqrt(np.mean(t * t, axis=-1, keepdims=True) + EPS)) * g


def grid_angles(fa):
    cf = C - 2 * (C // 3)
    ch = C // 3
    cw = C // 3
    af = fa[:GF, :cf]
    ah = fa[:GH, cf:cf + ch]
    aw = fa[:GW, cf + ch:C]
    ang = np.concatenate([
        np.broadcast_to(af[:, None, None, :], (GF, GH, GW, cf)),
        np.broadcast_to(ah[None, :, None, :], (GF, GH, GW, ch)),
        np.broadcast_to(aw[None, None, :, :], (GF, GH, GW, cw)),
    ], axis=-1)
    return ang.reshape(S, C)


def rope(t, cos, sin):
    te, to = t[..., 0::2], t[..., 1::2]
    return np.stack([te * cos - to * sin, te * sin + to * cos], axis=-1).reshape(t.shape)


def draw0():
    s = mx_kscale(DM)
    return {
        "x": bf(np.random.standard_normal((B, S, DM)) * s),
        "freqs_angle": bf(np.random.standard_normal((L, C))),
        "Wq": bf(np.random.standard_normal((DI, DM)) / np.sqrt(DM) / s[None, :]),
        "bq": bf(np.random.standard_normal(DI) * 0.2),
        "Wk": bf(np.random.standard_normal((DI, DM)) / np.sqrt(DM) / s[None, :]),
        "bk": bf(np.random.standard_normal(DI) * 0.2),
        "gq": bf(1.0 + 0.1 * np.random.standard_normal(DI)),
        "gk": bf(1.0 + 0.1 * np.random.standard_normal(DI)),
    }


def core(x, freqs_angle, Wq, bq, Wk, bk, gq, gk):
    ang = grid_angles(f64(freqs_angle))
    cos = np.cos(ang)[None, :, None, :]
    sin = np.sin(ang)[None, :, None, :]
    xq = mxq(f64(x), 2, "e4m3")
    tq = (xq @ mxq(f64(Wq), 1, "e4m3").T) + f64(bq)
    tk = (xq @ mxq(f64(Wk), 1, "e4m3").T) + f64(bk)
    q = rms(tq, f64(gq)).reshape(B, S, NH, HD)
    k = rms(tk, f64(gk)).reshape(B, S, NH, HD)
    return rope(q, cos, sin), rope(k, cos, sin)


def e4m3fn_bytes(y):
    return np.clip(np.asarray(y, np.float64), -448.0, 448.0).astype(np.float32).astype(ml_dtypes.float8_e4m3fn).view(np.uint8)


def e4m3fn_values(b):
    return np.asarray(b, np.uint8).view(ml_dtypes.float8_e4m3fn).astype(np.float64)


def setup_inputs():
    d = draw0()
    x0 = np.asarray(d['Wq']).astype(np.float64)
    s = (np.max(np.abs(x0), axis=(0,), keepdims=True) / 448.0).astype(np.float32)
    out = {}
    for k, v in d.items():
        if k == 'Wq':
            out['Wq_bytes'] = e4m3fn_bytes(x0 / s.astype(np.float64))
            out['Wq_scale'] = s
        else:
            out[k] = v
    return out


def reference(x, freqs_angle, Wq_bytes, Wq_scale, bq, Wk, bk, gq, gk):
    return core(x, freqs_angle, e4m3fn_values(Wq_bytes) * Wq_scale.astype(np.float64), bq, Wk, bk, gq, gk)

@@ -1,0 +1,310 @@
+from contextlib import ExitStack
+
+import concourse.mybir as mybir
+from concourse.masks import make_identity
+
+F32 = mybir.dt.float32
+BF16 = mybir.dt.bfloat16
+U32 = mybir.dt.uint32
+U8 = mybir.dt.uint8
+I32 = mybir.dt.int32
+FP8 = mybir.dt.float8_e4m3fn
+FP8X4 = mybir.dt.float8_e4m3fn_x4
+ACT = mybir.ActivationFunctionType
+ALU = mybir.AluOpType
+AX = mybir.AxisListType
+
+S_TOK = 512
+DM = 2048
+DI = 2048
+NH = 16
+EPS = 1e-6
+FLOPS = 2 * S_TOK * DM * (2 * DI)
+
+P = 128
+NPRE = 12
+IMM = 2
+PI = 3.141592653589793
+TWO_PI = 2.0 * PI
+C1 = 6.28125
+C2 = TWO_PI - C1
+SUM_GROUPS = {"k": [[0, 1, 2, 3], [4, 5, 6, 7], [8, 9, 10, 11], [12, 13, 14, 15]],
+              "q": [[0, 1, 2, 3], [4, 5, 6, 7], [8, 9, 10, 11], [12, 13, 14], [15]]}
+
+
+def tile_simpleselfattention_pa_kernel(tc, x, freqs_angle, Wq_bytes, Wq_scale, bq, Wk, bk, gq, gk, out_0, out_1):
+    nc = tc.nc
+    xf = x.rearrange("b s k -> (b s) k")
+    outs = {"q": out_0.rearrange("b s h d -> (b s) (h d)"), "k": out_1.rearrange("b s h d -> (b s) (h d)")}
+
+    with ExitStack() as ctx:
+        const = ctx.enter_context(tc.tile_pool(name="const", bufs=1))
+        raw = ctx.enter_context(tc.tile_pool(name="raw", bufs=6))
+        byt = ctx.enter_context(tc.tile_pool(name="byt", bufs=4))
+        prod = ctx.enter_context(tc.tile_pool(name="prod", bufs=NPRE))
+        grp = ctx.enter_context(tc.tile_pool(name="grp", bufs=4))
+        cod = ctx.enter_context(tc.tile_pool(name="cod", bufs=5))
+        upool = ctx.enter_context(tc.tile_pool(name="upool", bufs=28))
+        sqpool = ctx.enter_context(tc.tile_pool(name="sqpool", bufs=8))
+        jpool = ctx.enter_context(tc.tile_pool(name="jpool", bufs=2))
+        mpool = ctx.enter_context(tc.tile_pool(name="mpool", bufs=8))
+        m2pool = ctx.enter_context(tc.tile_pool(name="m2pool", bufs=3))
+        ps_t = ctx.enter_context(tc.psum_pool(name="ps_t", bufs=3))
+        ps_a = ctx.enter_context(tc.psum_pool(name="ps_a", bufs=2))
+        ps_f = ctx.enter_context(tc.psum_pool(name="ps_f", bufs=3))
+
+        def load_rows(dram_rows):
+            t = raw.tile([P, DM], BF16, name="wraw", tag="wraw")
+            nc.sync.dma_start(out=t[:], in_=dram_rows)
+            return t
+
+        def load_q8(j):
+            t = byt.tile([P, DM], U8, name="wq8", tag="wq8")
+            nc.sync.dma_start(out=t[:], in_=Wq_bytes[P * j:P * (j + 1), :])
+            return t
+
+        vb = const.tile([P, P], BF16, name="vb")
+        nc.vector.memset(vb[:], 0.0)
+        for r, v in enumerate((bq, bk, gq, gk)):
+            nc.sync.dma_start(out=vb[16 * r:16 * (r + 1), :], in_=v.rearrange("(h p) -> h p", p=P))
+        xraw = [load_rows(xf[P * i:P * (i + 1), :]) for i in range(4)]
+        src = {}
+        q8 = {}
+        src[0] = load_rows(Wk[0:P, :])
+        src[1] = load_rows(Wk[P:2 * P, :])
+        scale_bc = const.tile([P, DM], F32, name="scale_bc")
+        nc.sync.dma_start(out=scale_bc[:], in_=Wq_scale.rearrange("o k -> (o k)").partition_broadcast(P))
+        q8[0] = load_q8(0)
+
+        ident = const.tile([P, P], F32, name="ident")
+        make_identity(nc, ident[:])
+        mhalf = const.tile([P, 4], F32, name="mhalf")
+        nc.gpsimd.memset(mhalf[:], -0.5)
+
+        faf = const.tile([P, 256], BF16, name="faf")
+        nc.gpsimd.dma_start(out=faf[:], in_=freqs_angle[0:4, :].rearrange("a j -> (a j)").partition_broadcast(P))
+        fah = const.tile([P, 64], BF16, name="fah")
+        faw = const.tile([P, 64], BF16, name="faw")
+        for h in range(8):
+            nc.gpsimd.dma_start(out=fah[16 * h:16 * (h + 1), :],
+                                in_=freqs_angle[h:h + 1, :].rearrange("o j -> (o j)").partition_broadcast(16))
+            nc.gpsimd.dma_start(out=faw[16 * h:16 * (h + 1), :], in_=freqs_angle[0:16, :])
+
+        def flip_in(rows, dst, dst_g, on_vector):
+            words = rows[:].bitcast(F32)
+            for half in range(2):
+                tp = ps_t.tile([P, 4, P], F32, name="tp", tag="tp")
+                for gl in range(2):
+                    g = 2 * half + gl
+                    for u in range(2):
+                        nc.tensor.transpose(tp[:, 2 * gl + u, :], words[:, 256 * g + u:256 * (g + 1):2], ident[:])
+                copy = nc.vector.tensor_copy if on_vector[half] else nc.scalar.copy
+                if dst_g is None:
+                    copy(out=dst[:, 2 * half:2 * half + 2, :, :], in_=tp[:].rearrange("p (gl u) r -> p gl r u", u=2))
+                else:
+                    for gl in range(2):
+                        copy(out=dst_g[2 * half + gl], in_=tp[:, 2 * gl:2 * gl + 2, :].rearrange("p u r -> p r u"))
+
+        xg = [prod.tile([P, DM], BF16, name="wprod", tag="wprod", align_bytes=64) for g in range(4)]
+        xgw = [xg[g][:].bitcast(F32).rearrange("p (s u) -> p s u", u=2) for g in range(4)]
+        xc = const.tile([P, 4, S_TOK], U32, name="xc", align_bytes=64)
+        xs = const.tile([P, 4, S_TOK], U8, name="xs", align_bytes=64)
+        for i in range(4):
+            flip_in(xraw[i], None, [xgw[g][:, P * i:P * (i + 1), :] for g in range(4)], (False, True))
+        for g in range(4):
+            nc.vector.quantize_mx(out=xc[:, g, :].bitcast(FP8X4), scales=xs[:, g, :], in_=xg[g][:])
+
+        vf = const.tile([P, P], F32, name="vf")
+        nc.vector.tensor_copy(out=vf[:], in_=vb[:])
+        tpv = ps_t.tile([P, 4, P], F32, name="tp", tag="tp")
+        nc.tensor.transpose(tpv[:, 0, :], vf[:], ident[:])
+        cols = const.tile([P, P], F32, name="cols")
+        nc.vector.tensor_copy(out=cols[:], in_=tpv[:, 0, :])
+        gb = const.tile([P, 32], F32, name="gb")
+        nc.vector.tensor_tensor(out=gb[:], in0=cols[:, 0:32], in1=cols[:, 32:64], op=ALU.mult)
+
+        def product(t8):
+            w = prod.tile([P, DM], BF16, name="wprod", tag="wprod", align_bytes=64)
+            nc.vector.tensor_tensor(out=w[:], in0=t8[:].bitcast(FP8), in1=scale_bc[:], op=ALU.mult)
+            return w
+
+        def flip_head(rows):
+            gw = grp.tile([P, DM], BF16, name="gw", tag="gw", align_bytes=64)
+            flip_in(rows, gw[:].bitcast(F32).rearrange("p (g r u) -> p g r u", g=4, u=2), None, (False, False))
+            return gw
+
+        def quant_head(gw):
+            wc = cod.tile([P, 512], U32, name="wc", tag="wc", align_bytes=64)
+            ws = cod.tile([P, 512], U8, name="ws", tag="ws", align_bytes=64)
+            nc.vector.quantize_mx(out=wc[:].bitcast(FP8X4), scales=ws[:], in_=gw[:])
+            return wc, ws
+
+        def mx_head(wc, ws, col):
+            acc = ps_a.tile([P, S_TOK], F32, name="acc", tag="acc")
+            for g in range(4):
+                nc.tensor.matmul_mx(out=acc[:], lhsT=wc[:, P * g:P * (g + 1)].bitcast(FP8X4), lhsT_scale=ws[:, P * g:P * (g + 1)],
+                                    rhs=xc[:, g, :].bitcast(FP8X4), rhs_scale=xs[:, g, :], start=(g == 0), stop=(g == 3))
+            sq = sqpool.tile([P, S_TOK], F32, name="sq", tag="sq")
+            nc.scalar.activation(out=sq[:], in_=acc[:], func=ACT.Square, bias=cols[:, col:col + 1], scale=1.0)
+            u = upool.tile([P, S_TOK], F32, name="u", tag="u")
+            nc.scalar.activation(out=u[:], in_=acc[:], func=ACT.Identity, bias=gb[:, col:col + 1], scale=cols[:, 32 + col:33 + col])
+            return u, sq
+
+        ss = {"q": const.tile([P, 4, 5], F32, name="ss_q"), "k": const.tile([P, 4, 5], F32, name="ss_k")}
+
+        def sumsq(kind, gi, sqn):
+            fl = ps_f.tile([P, 4, P], F32, name="fl", tag="fl")
+            for i in range(4):
+                for a in range(len(sqn)):
+                    nc.tensor.matmul(out=fl[:, i, :], lhsT=sqn[a][:, P * i:P * (i + 1)], rhs=ident[:], is_transpose=True,
+                                     start=(a == 0), stop=(a == len(sqn) - 1))
+            for i in range(4):
+                junk = jpool.tile([P, P], BF16, name="junk", tag="junk")
+                nc.scalar.activation(out=junk[:], in_=fl[:, i, :], func=ACT.Copy, accum_out=ss[kind][:, i, gi:gi + 1])
+
+        def norm(kind):
+            tot = const.tile([P, 4], F32, name="tot_" + kind)
+            nc.vector.tensor_reduce(out=tot[:], in_=ss[kind][:, :, 0:len(SUM_GROUPS[kind])], axis=AX.X, op=ALU.add)
+            nc.vector.tensor_scalar(out=tot[:], in0=tot[:], scalar1=1.0 / DI, scalar2=EPS, op0=ALU.mult, op1=ALU.add)
+            rr = const.tile([P, 4], F32, name="rr_" + kind)
+            nc.gpsimd.tensor_tensor(out=rr[:], in0=tot[:], in1=mhalf[:], op=ALU.pow)
+            return rr
+
+        NA = 130
+        ang = const.tile([P, 2, NA], F32, name="ang")
+        angf = ang[:].rearrange("p c n -> p (c n)")
+        ki = const.tile([P, 2 * NA], I32, name="ki")
+        kf = const.tile([P, 2 * NA], F32, name="kf")
+        yy = const.tile([P, 2 * NA], F32, name="yy")
+        msk = const.tile([P, 2 * NA], F32, name="msk")
+        sc = const.tile([P, 2, NA], F32, name="sc")
+        cs = const.tile([P, 2, 4, P], F32, name="cs")
+        cs5 = cs[:].rearrange("p c a (j e) -> p c a j e", e=2)
+
+        def trig_a():
+            nc.vector.tensor_copy(out=ang[:, 0, 0:88].rearrange("p (a j) -> p a j", a=4),
+                                  in_=faf[:].rearrange("p (a j) -> p a j", a=4)[:, :, 0:22])
+            nc.vector.tensor_copy(out=ang[:, 0, 88:109], in_=fah[:, 22:43])
+            nc.vector.tensor_copy(out=ang[:, 0, 109:130], in_=faw[:, 43:64])
+            nc.vector.tensor_scalar(out=ang[:, 1, :], in0=ang[:, 0, :], scalar1=0.5 * PI, scalar2=None, op0=ALU.add)
+            nc.vector.tensor_scalar(out=ki[:], in0=angf, scalar1=1.0 / TWO_PI, scalar2=None, op0=ALU.mult)
+            nc.vector.tensor_copy(out=kf[:], in_=ki[:])
+            nc.vector.scalar_tensor_tensor(out=yy[:], in0=kf[:], scalar=-C1, in1=angf, op0=ALU.mult, op1=ALU.add)
+            nc.vector.scalar_tensor_tensor(out=yy[:], in0=kf[:], scalar=-C2, in1=yy[:], op0=ALU.mult, op1=ALU.add)
+            nc.vector.tensor_scalar(out=msk[:], in0=yy[:], scalar1=PI, scalar2=None, op0=ALU.is_gt)
+            nc.vector.scalar_tensor_tensor(out=yy[:], in0=msk[:], scalar=-TWO_PI, in1=yy[:], op0=ALU.mult, op1=ALU.add)
+            nc.vector.tensor_scalar(out=msk[:], in0=yy[:], scalar1=-PI, scalar2=None, op0=ALU.is_lt)
+            nc.vector.scalar_tensor_tensor(out=yy[:], in0=msk[:], scalar=TWO_PI, in1=yy[:], op0=ALU.mult, op1=ALU.add)
+
+        def trig_b():
+            nc.scalar.activation(out=sc[:].rearrange("p c n -> p (c n)"), in_=yy[:], func=ACT.Sin)
+            for c in range(2):
+                s_ = 1 - c
+                nc.gpsimd.tensor_copy(out=cs5[:, c, :, 0:22, :],
+                                      in_=sc[:, s_, 0:88].rearrange("p (a j) -> p a j", a=4).unsqueeze(3).to_broadcast([P, 4, 22, 2]))
+                nc.gpsimd.tensor_copy(out=cs5[:, c, :, 22:43, :],
+                                      in_=sc[:, s_, 88:109].unsqueeze(1).unsqueeze(3).to_broadcast([P, 4, 21, 2]))
+                nc.gpsimd.tensor_copy(out=cs5[:, c, :, 43:64, :],
+                                      in_=sc[:, s_, 109:130].unsqueeze(1).unsqueeze(3).to_broadcast([P, 4, 21, 2]))
+            nc.gpsimd.tensor_scalar(out=cs5[:, 1, :, :, 0], in0=cs5[:, 1, :, :, 0], scalar1=-1.0, scalar2=0.0,
+                                    op0=ALU.mult, op1=ALU.add)
+
+        trig_at = {14: trig_a, 16: trig_b}
+
+        def rope_flips(i, u4):
+            fu = ps_f.tile([P, 4, P], F32, name="fl", tag="fl")
+            for a in range(4):
+                nc.tensor.transpose(fu[:, a, :], u4[a][:, P * i:P * (i + 1)], ident[:])
+            return fu
+
+        def rope_unit(i, fu, rr, adder):
+            if rr is None:
+                m1 = upool.tile([P, S_TOK], F32, name="u", tag="u")
+            else:
+                m1 = mpool.tile([P, S_TOK], F32, name="m1", tag="m1")
+            m2 = m2pool.tile([P, S_TOK], F32, name="m2", tag="m2")
+            o1 = m1[:].rearrange("p (a n) -> p a n", a=4)
+            c1 = cs[:, 0, i, :].unsqueeze(1).to_broadcast([P, 4, P])
+            o2 = m2[:].rearrange("p (a j e) -> p a j e", a=4, e=2)
+            f2 = fu[:].rearrange("p a (j e) -> p a j e", e=2)[:, :, :, ::-1]
+            c2 = cs[:, 1, i, :].rearrange("p (j e) -> p j e", e=2).unsqueeze(1).to_broadcast([P, 4, 64, 2])
+            if rr is None:
+                nc.vector.tensor_tensor(out=o1, in0=fu[:], in1=c1, op=ALU.mult)
+                nc.vector.tensor_tensor(out=o2, in0=f2, in1=c2, op=ALU.mult)
+            else:
+                nc.vector.scalar_tensor_tensor(out=o1, in0=fu[:], scalar=rr[:, i:i + 1], in1=c1, op0=ALU.mult, op1=ALU.mult)
+                nc.vector.scalar_tensor_tensor(out=o2, in0=f2, scalar=rr[:, i:i + 1], in1=c2, op0=ALU.mult, op1=ALU.mult)
+            adder.tensor_tensor(out=m1[:], in0=m1[:], in1=m2[:], op=ALU.add)
+            return m1
+
+        def store(queue, kind, i, gi, m1):
+            queue.dma_start(out=outs[kind][P * i:P * (i + 1), 512 * gi:512 * (gi + 1)], in_=m1[:])
+
+        heads = [("k", j) for j in range(NH)] + [("q", j) for j in range(NH)]
+        N = len(heads)
+        prod_at = {}
+        for j in range(NH):
+            st = j + 2 if j < NPRE else max(17 + j - NPRE, j + 2)
+            prod_at.setdefault(st, []).append(j)
+            if j > 0:
+                prod_at.setdefault(("load", max(st - 2, 0)), []).append(j)
+        gws = {}
+        cds = {}
+        us = {"q": [], "k": []}
+        sqs = {"q": [], "k": []}
+        rrs = {}
+        ready = []
+        taken = 0
+        early = []
+        for s in range(N + 4):
+            n_units = 0 if s < 19 else (1 if s < 23 or s % 2 == 0 else 2)
+            todo = ready[taken:taken + n_units]
+            taken += len(todo)
+            fus = [rope_flips(i, us[kind][4 * gi:4 * gi + 4]) for kind, i, gi in todo]
+            if s + 2 < NH:
+                src[s + 2] = load_rows(Wk[P * (s + 2):P * (s + 3), :])
+            for j in prod_at.get(("load", s), []):
+                q8[j] = load_q8(j)
+            if s < N:
+                gws[s] = flip_head(src[s])
+            if 0 <= s - 1 < N:
+                cds[s - 1] = quant_head(gws[s - 1])
+            for j in prod_at.get(s, []):
+                src[NH + j] = product(q8[j])
+            if 0 <= s - 3 < N:
+                kind, j = heads[s - 3]
+                u, sq = mx_head(cds[s - 3][0], cds[s - 3][1], j if kind == "q" else NH + j)
+                us[kind].append(u)
+                sqs[kind].append(sq)
+                if kind == "q" and j % 4 == 3 and j // 4 < IMM:
+                    ready.extend([("q", i, j // 4) for i in range(4)])
+            for (kind, i, gi), fu in zip(todo, fus):
+                if kind == "k":
+                    store(nc.sync, "k", i, gi, rope_unit(i, fu, rrs["k"], nc.gpsimd))
+                else:
+                    early.append((i, gi, rope_unit(i, fu, None, nc.gpsimd)))
+            if s in trig_at:
+                trig_at[s]()
+            if s - 4 >= 0:
+                kind, j = heads[s - 4]
+                for gi, hs in enumerate(SUM_GROUPS[kind]):
+                    if hs[-1] == j:
+                        sumsq(kind, gi, [sqs[kind][h] for h in hs])
+                if j == NH - 1:
+                    rrs[kind] = norm(kind)
+                    if kind == "k":
+                        ready.extend([("k", i, gi) for gi in range(4) for i in range(4)])
+
+        for kind, i, gi in ready[taken:]:
+            fu = rope_flips(i, us[kind][4 * gi:4 * gi + 4])
+            if kind == "k":
+                store(nc.sync, "k", i, gi, rope_unit(i, fu, rrs["k"], nc.gpsimd))
+            else:
+                early.append((i, gi, rope_unit(i, fu, None, nc.gpsimd)))
+        for i, gi, m1 in early:
+            nc.scalar.activation(out=m1[:], in_=m1[:], func=ACT.Copy, scale=rrs["q"][:, i:i + 1])
+            store(nc.scalar, "q", i, gi, m1)
+        for gi in range(IMM, 4):
+            for i in range(4):
+                last = (gi == 3 and i == 3)
+                store(nc.sync, "q", i, gi, rope_unit(i, rope_flips(i, us["q"][4 * gi:4 * gi + 4]), rrs["q"], nc.vector if last else nc.gpsimd))

@@ -67,6 +67,9 @@ def tile_simpleselfattention_pa_kernel(tc, x, freqs_angle, Wq_bytes, Wq_scale, b
         nc.vector.memset(vb[:], 0.0)
         for r, v in enumerate((bq, bk, gq, gk)):
             nc.sync.dma_start(out=vb[16 * r:16 * (r + 1), :], in_=v.rearrange("(h p) -> h p", p=P))
+        fr = const.tile([P, 64], BF16, name="fr")
+        nc.vector.memset(fr[:], 0.0)
+        nc.sync.dma_start(out=fr[0:16, :], in_=freqs_angle[0:16, :])
         xraw = [load_rows(xf[P * i:P * (i + 1), :]) for i in range(4)]
         src = {}
         q8 = {}
@@ -81,14 +84,24 @@ def tile_simpleselfattention_pa_kernel(tc, x, freqs_angle, Wq_bytes, Wq_scale, b
         mhalf = const.tile([P, 4], F32, name="mhalf")
         nc.gpsimd.memset(mhalf[:], -0.5)
 
-        faf = const.tile([P, 256], BF16, name="faf")
-        nc.gpsimd.dma_start(out=faf[:], in_=freqs_angle[0:4, :].rearrange("a j -> (a j)").partition_broadcast(P))
-        fah = const.tile([P, 64], BF16, name="fah")
-        faw = const.tile([P, 64], BF16, name="faw")
-        for h in range(8):
-            nc.gpsimd.dma_start(out=fah[16 * h:16 * (h + 1), :],
-                                in_=freqs_angle[h:h + 1, :].rearrange("o j -> (o j)").partition_broadcast(16))
-            nc.gpsimd.dma_start(out=faw[16 * h:16 * (h + 1), :], in_=freqs_angle[0:16, :])
+        identb = const.tile([P, P], BF16, name="identb")
+        make_identity(nc, identb[:])
+        selh = const.tile([P, 8, 16], BF16, name="selh")
+        selw = const.tile([P, 8, 16], BF16, name="selw")
+        nc.vector.tensor_copy(out=selh[:], in_=identb[:, 0:8].unsqueeze(2).to_broadcast([P, 8, 16]))
+        nc.vector.tensor_copy(out=selw[:], in_=identb[:, 0:16].unsqueeze(1).to_broadcast([P, 8, 16]))
+        pa = ps_t.tile([P, 4, P], F32, name="tp", tag="tp")
+        paf = pa[:].rearrange("p a n -> p (a n)")
+        for a in range(4):
+            nc.tensor.matmul(out=paf[:, 64 * a:64 * (a + 1)], lhsT=identb[:, a:a + 1].to_broadcast([P, P]), rhs=fr[:], start=True, stop=True)
+        nc.tensor.matmul(out=paf[:, 256:320], lhsT=selh[:].rearrange("p h w -> p (h w)"), rhs=fr[:], start=True, stop=True)
+        nc.tensor.matmul(out=paf[:, 320:384], lhsT=selw[:].rearrange("p h w -> p (h w)"), rhs=fr[:], start=True, stop=True)
+        NA = 130
+        ang = const.tile([P, 2, NA], F32, name="ang")
+        nc.vector.tensor_copy(out=ang[:, 0, 0:88].rearrange("p (a j) -> p a j", a=4),
+                              in_=paf[:, 0:256].rearrange("p (a j) -> p a j", a=4)[:, :, 0:22])
+        nc.vector.tensor_copy(out=ang[:, 0, 88:109], in_=paf[:, 278:299])
+        nc.vector.tensor_copy(out=ang[:, 0, 109:130], in_=paf[:, 363:384])
 
         def flip_in(rows, dst, dst_g, on_vector):
             words = rows[:].bitcast(F32)
@@ -170,8 +183,6 @@ def tile_simpleselfattention_pa_kernel(tc, x, freqs_angle, Wq_bytes, Wq_scale, b
             nc.gpsimd.tensor_tensor(out=rr[:], in0=tot[:], in1=mhalf[:], op=ALU.pow)
             return rr
 
-        NA = 130
-        ang = const.tile([P, 2, NA], F32, name="ang")
         angf = ang[:].rearrange("p c n -> p (c n)")
         ki = const.tile([P, 2 * NA], I32, name="ki")
         kf = const.tile([P, 2 * NA], F32, name="kf")
@@ -182,10 +193,6 @@ def tile_simpleselfattention_pa_kernel(tc, x, freqs_angle, Wq_bytes, Wq_scale, b
         cs5 = cs[:].rearrange("p c a (j e) -> p c a j e", e=2)
 
         def trig_a():
-            nc.vector.tensor_copy(out=ang[:, 0, 0:88].rearrange("p (a j) -> p a j", a=4),
-                                  in_=faf[:].rearrange("p (a j) -> p a j", a=4)[:, :, 0:22])
-            nc.vector.tensor_copy(out=ang[:, 0, 88:109], in_=fah[:, 22:43])
-            nc.vector.tensor_copy(out=ang[:, 0, 109:130], in_=faw[:, 43:64])
             nc.vector.tensor_scalar(out=ang[:, 1, :], in0=ang[:, 0, :], scalar1=0.5 * PI, scalar2=None, op0=ALU.add)
             nc.vector.tensor_scalar(out=ki[:], in0=angf, scalar1=1.0 / TWO_PI, scalar2=None, op0=ALU.mult)
             nc.vector.tensor_copy(out=kf[:], in_=ki[:])
@@ -209,7 +216,9 @@ def tile_simpleselfattention_pa_kernel(tc, x, freqs_angle, Wq_bytes, Wq_scale, b
             nc.gpsimd.tensor_scalar(out=cs5[:, 1, :, :, 0], in0=cs5[:, 1, :, :, 0], scalar1=-1.0, scalar2=0.0,
                                     op0=ALU.mult, op1=ALU.add)
 
-        trig_at = {14: trig_a, 16: trig_b}
+        trig_a()
+        trig_b()
+        trig_at = {}
 
         def rope_flips(i, u4):
             fu = ps_f.tile([P, 4, P], F32, name="fl", tag="fl")

@@ -249,6 +249,7 @@ def tile_simpleselfattention_pa_kernel(tc, x, freqs_angle, Wq_bytes, Wq_scale, b
         def store(queue, kind, i, gi, m1):
             queue.dma_start(out=outs[kind][P * i:P * (i + 1), 512 * gi:512 * (gi + 1)], in_=m1[:])
 
+        ctx.enter_context(tc.manual_schedule())
         heads = [("k", j) for j in range(NH)] + [("q", j) for j in range(NH)]
         N = len(heads)
         prod_at = {}

@@ -53,6 +53,10 @@ def tile_simpleselfattention_pa_kernel(tc, x, freqs_angle, Wq_bytes, Wq_scale, b
         ps_a = ctx.enter_context(tc.psum_pool(name="ps_a", bufs=2))
         ps_f = ctx.enter_context(tc.psum_pool(name="ps_f", bufs=3))
 
+        warm = const.tile([P, 1], F32, name="warm")
+        nc.gpsimd.memset(warm[:], 0.0)
+        nc.scalar.activation(out=warm[:], in_=warm[:], func=ACT.Sin)
+
         def load_rows(dram_rows):
             t = raw.tile([P, DM], BF16, name="wraw", tag="wraw")
             nc.sync.dma_start(out=t[:], in_=dram_rows)
@@ -175,6 +179,14 @@ def tile_simpleselfattention_pa_kernel(tc, x, freqs_angle, Wq_bytes, Wq_scale, b
                 junk = jpool.tile([P, P], BF16, name="junk", tag="junk")
                 nc.scalar.activation(out=junk[:], in_=fl[:, i, :], func=ACT.Copy, accum_out=ss[kind][:, i, gi:gi + 1])
 
+        def sumsq_part(kind, gi, sqn, i):
+            fp = ps_t.tile([P, 4, P], F32, name="tp", tag="tp")
+            for a in range(len(sqn)):
+                nc.tensor.matmul(out=fp[:, 0, :], lhsT=sqn[a][:, P * i:P * (i + 1)], rhs=ident[:], is_transpose=True,
+                                 start=(a == 0), stop=(a == len(sqn) - 1))
+            junk = jpool.tile([P, P], BF16, name="junk", tag="junk")
+            nc.scalar.activation(out=junk[:], in_=fp[:, 0, :], func=ACT.Copy, accum_out=ss[kind][:, i, gi:gi + 1])
+
         def norm(kind):
             tot = const.tile([P, 4], F32, name="tot_" + kind)
             nc.vector.tensor_reduce(out=tot[:], in_=ss[kind][:, :, 0:len(SUM_GROUPS[kind])], axis=AX.X, op=ALU.add)
@@ -263,6 +275,7 @@ def tile_simpleselfattention_pa_kernel(tc, x, freqs_angle, Wq_bytes, Wq_scale, b
         us = {"q": [], "k": []}
         sqs = {"q": [], "k": []}
         rrs = {}
+        parts = {}
         ready = []
         taken = 0
         early = []
@@ -298,8 +311,13 @@ def tile_simpleselfattention_pa_kernel(tc, x, freqs_angle, Wq_bytes, Wq_scale, b
             if s - 4 >= 0:
                 kind, j = heads[s - 4]
                 for gi, hs in enumerate(SUM_GROUPS[kind]):
-                    if hs[-1] == j:
+                    if hs[-1] == j and gi < 3:
+                        for i in range(4):
+                            parts.setdefault(s + i, []).append((kind, gi, hs, i))
+                    elif hs[-1] == j:
                         sumsq(kind, gi, [sqs[kind][h] for h in hs])
+                for pk, gi, hs, i in parts.get(s, []):
+                    sumsq_part(pk, gi, [sqs[pk][h] for h in hs], i)
                 if j == NH - 1:
                     rrs[kind] = norm(kind)
                     if kind == "k":

from contextlib import ExitStack

import concourse.mybir as mybir
from concourse.masks import make_identity

F32 = mybir.dt.float32
BF16 = mybir.dt.bfloat16
U32 = mybir.dt.uint32
U8 = mybir.dt.uint8
I32 = mybir.dt.int32
FP8 = mybir.dt.float8_e4m3fn
FP8X4 = mybir.dt.float8_e4m3fn_x4
ACT = mybir.ActivationFunctionType
ALU = mybir.AluOpType
AX = mybir.AxisListType

S_TOK = 512
DM = 2048
DI = 2048
NH = 16
EPS = 1e-6
FLOPS = 2 * S_TOK * DM * (2 * DI)

P = 128
NPRE = 12
IMM = 2
PI = 3.141592653589793
TWO_PI = 2.0 * PI
C1 = 6.28125
C2 = TWO_PI - C1
SUM_GROUPS = {"k": [[0, 1, 2, 3], [4, 5, 6, 7], [8, 9, 10, 11], [12, 13, 14, 15]],
              "q": [[0, 1, 2, 3], [4, 5, 6, 7], [8, 9, 10, 11], [12, 13, 14], [15]]}


def tile_simpleselfattention_pa_kernel(tc, x, freqs_angle, Wq_bytes, Wq_scale, bq, Wk, bk, gq, gk, out_0, out_1):
    nc = tc.nc
    xf = x.rearrange("b s k -> (b s) k")
    outs = {"q": out_0.rearrange("b s h d -> (b s) (h d)"), "k": out_1.rearrange("b s h d -> (b s) (h d)")}

    with ExitStack() as ctx:
        const = ctx.enter_context(tc.tile_pool(name="const", bufs=1))
        raw = ctx.enter_context(tc.tile_pool(name="raw", bufs=6))
        byt = ctx.enter_context(tc.tile_pool(name="byt", bufs=4))
        prod = ctx.enter_context(tc.tile_pool(name="prod", bufs=NPRE))
        grp = ctx.enter_context(tc.tile_pool(name="grp", bufs=4))
        cod = ctx.enter_context(tc.tile_pool(name="cod", bufs=5))
        upool = ctx.enter_context(tc.tile_pool(name="upool", bufs=28))
        sqpool = ctx.enter_context(tc.tile_pool(name="sqpool", bufs=8))
        jpool = ctx.enter_context(tc.tile_pool(name="jpool", bufs=2))
        mpool = ctx.enter_context(tc.tile_pool(name="mpool", bufs=8))
        m2pool = ctx.enter_context(tc.tile_pool(name="m2pool", bufs=3))
        ps_t = ctx.enter_context(tc.psum_pool(name="ps_t", bufs=3))
        ps_a = ctx.enter_context(tc.psum_pool(name="ps_a", bufs=2))
        ps_f = ctx.enter_context(tc.psum_pool(name="ps_f", bufs=3))

        warm = const.tile([P, 1], F32, name="warm")
        nc.gpsimd.memset(warm[:], 0.0)
        nc.scalar.activation(out=warm[:], in_=warm[:], func=ACT.Sin)

        def load_rows(dram_rows):
            t = raw.tile([P, DM], BF16, name="wraw", tag="wraw")
            nc.sync.dma_start(out=t[:], in_=dram_rows)
            return t

        def load_q8(j):
            t = byt.tile([P, DM], U8, name="wq8", tag="wq8")
            nc.sync.dma_start(out=t[:], in_=Wq_bytes[P * j:P * (j + 1), :])
            return t

        vb = const.tile([P, P], BF16, name="vb")
        nc.vector.memset(vb[:], 0.0)
        for r, v in enumerate((bq, bk, gq, gk)):
            nc.sync.dma_start(out=vb[16 * r:16 * (r + 1), :], in_=v.rearrange("(h p) -> h p", p=P))
        fr = const.tile([P, 64], BF16, name="fr")
        nc.vector.memset(fr[:], 0.0)
        nc.sync.dma_start(out=fr[0:16, :], in_=freqs_angle[0:16, :])
        xraw = [load_rows(xf[P * i:P * (i + 1), :]) for i in range(4)]
        src = {}
        q8 = {}
        src[0] = load_rows(Wk[0:P, :])
        src[1] = load_rows(Wk[P:2 * P, :])
        scale_bc = const.tile([P, DM], F32, name="scale_bc")
        nc.sync.dma_start(out=scale_bc[:], in_=Wq_scale.rearrange("o k -> (o k)").partition_broadcast(P))
        q8[0] = load_q8(0)

        ident = const.tile([P, P], F32, name="ident")
        make_identity(nc, ident[:])
        mhalf = const.tile([P, 4], F32, name="mhalf")
        nc.gpsimd.memset(mhalf[:], -0.5)

        identb = const.tile([P, P], BF16, name="identb")
        make_identity(nc, identb[:])
        selh = const.tile([P, 8, 16], BF16, name="selh")
        selw = const.tile([P, 8, 16], BF16, name="selw")
        nc.vector.tensor_copy(out=selh[:], in_=identb[:, 0:8].unsqueeze(2).to_broadcast([P, 8, 16]))
        nc.vector.tensor_copy(out=selw[:], in_=identb[:, 0:16].unsqueeze(1).to_broadcast([P, 8, 16]))
        pa = ps_t.tile([P, 4, P], F32, name="tp", tag="tp")
        paf = pa[:].rearrange("p a n -> p (a n)")
        for a in range(4):
            nc.tensor.matmul(out=paf[:, 64 * a:64 * (a + 1)], lhsT=identb[:, a:a + 1].to_broadcast([P, P]), rhs=fr[:], start=True, stop=True)
        nc.tensor.matmul(out=paf[:, 256:320], lhsT=selh[:].rearrange("p h w -> p (h w)"), rhs=fr[:], start=True, stop=True)
        nc.tensor.matmul(out=paf[:, 320:384], lhsT=selw[:].rearrange("p h w -> p (h w)"), rhs=fr[:], start=True, stop=True)
        NA = 130
        ang = const.tile([P, 2, NA], F32, name="ang")
        nc.vector.tensor_copy(out=ang[:, 0, 0:88].rearrange("p (a j) -> p a j", a=4),
                              in_=paf[:, 0:256].rearrange("p (a j) -> p a j", a=4)[:, :, 0:22])
        nc.vector.tensor_copy(out=ang[:, 0, 88:109], in_=paf[:, 278:299])
        nc.vector.tensor_copy(out=ang[:, 0, 109:130], in_=paf[:, 363:384])

        def flip_in(rows, dst, dst_g, on_vector):
            words = rows[:].bitcast(F32)
            for half in range(2):
                tp = ps_t.tile([P, 4, P], F32, name="tp", tag="tp")
                for gl in range(2):
                    g = 2 * half + gl
                    for u in range(2):
                        nc.tensor.transpose(tp[:, 2 * gl + u, :], words[:, 256 * g + u:256 * (g + 1):2], ident[:])
                copy = nc.vector.tensor_copy if on_vector[half] else nc.scalar.copy
                if dst_g is None:
                    copy(out=dst[:, 2 * half:2 * half + 2, :, :], in_=tp[:].rearrange("p (gl u) r -> p gl r u", u=2))
                else:
                    for gl in range(2):
                        copy(out=dst_g[2 * half + gl], in_=tp[:, 2 * gl:2 * gl + 2, :].rearrange("p u r -> p r u"))

        xg = [prod.tile([P, DM], BF16, name="wprod", tag="wprod", align_bytes=64) for g in range(4)]
        xgw = [xg[g][:].bitcast(F32).rearrange("p (s u) -> p s u", u=2) for g in range(4)]
        xc = const.tile([P, 4, S_TOK], U32, name="xc", align_bytes=64)
        xs = const.tile([P, 4, S_TOK], U8, name="xs", align_bytes=64)
        for i in range(4):
            flip_in(xraw[i], None, [xgw[g][:, P * i:P * (i + 1), :] for g in range(4)], (False, True))
        for g in range(4):
            nc.vector.quantize_mx(out=xc[:, g, :].bitcast(FP8X4), scales=xs[:, g, :], in_=xg[g][:])

        vf = const.tile([P, P], F32, name="vf")
        nc.vector.tensor_copy(out=vf[:], in_=vb[:])
        tpv = ps_t.tile([P, 4, P], F32, name="tp", tag="tp")
        nc.tensor.transpose(tpv[:, 0, :], vf[:], ident[:])
        cols = const.tile([P, P], F32, name="cols")
        nc.vector.tensor_copy(out=cols[:], in_=tpv[:, 0, :])
        gb = const.tile([P, 32], F32, name="gb")
        nc.vector.tensor_tensor(out=gb[:], in0=cols[:, 0:32], in1=cols[:, 32:64], op=ALU.mult)

        def product(t8):
            w = prod.tile([P, DM], BF16, name="wprod", tag="wprod", align_bytes=64)
            nc.vector.tensor_tensor(out=w[:], in0=t8[:].bitcast(FP8), in1=scale_bc[:], op=ALU.mult)
            return w

        def flip_head(rows):
            gw = grp.tile([P, DM], BF16, name="gw", tag="gw", align_bytes=64)
            flip_in(rows, gw[:].bitcast(F32).rearrange("p (g r u) -> p g r u", g=4, u=2), None, (False, False))
            return gw

        def quant_head(gw):
            wc = cod.tile([P, 512], U32, name="wc", tag="wc", align_bytes=64)
            ws = cod.tile([P, 512], U8, name="ws", tag="ws", align_bytes=64)
            nc.vector.quantize_mx(out=wc[:].bitcast(FP8X4), scales=ws[:], in_=gw[:])
            return wc, ws

        def mx_head(wc, ws, col):
            acc = ps_a.tile([P, S_TOK], F32, name="acc", tag="acc")
            for g in range(4):
                nc.tensor.matmul_mx(out=acc[:], lhsT=wc[:, P * g:P * (g + 1)].bitcast(FP8X4), lhsT_scale=ws[:, P * g:P * (g + 1)],
                                    rhs=xc[:, g, :].bitcast(FP8X4), rhs_scale=xs[:, g, :], start=(g == 0), stop=(g == 3))
            sq = sqpool.tile([P, S_TOK], F32, name="sq", tag="sq")
            nc.scalar.activation(out=sq[:], in_=acc[:], func=ACT.Square, bias=cols[:, col:col + 1], scale=1.0)
            u = upool.tile([P, S_TOK], F32, name="u", tag="u")
            nc.scalar.activation(out=u[:], in_=acc[:], func=ACT.Identity, bias=gb[:, col:col + 1], scale=cols[:, 32 + col:33 + col])
            return u, sq

        ss = {"q": const.tile([P, 4, 5], F32, name="ss_q"), "k": const.tile([P, 4, 5], F32, name="ss_k")}

        def sumsq(kind, gi, sqn):
            fl = ps_f.tile([P, 4, P], F32, name="fl", tag="fl")
            for i in range(4):
                for a in range(len(sqn)):
                    nc.tensor.matmul(out=fl[:, i, :], lhsT=sqn[a][:, P * i:P * (i + 1)], rhs=ident[:], is_transpose=True,
                                     start=(a == 0), stop=(a == len(sqn) - 1))
            for i in range(4):
                junk = jpool.tile([P, P], BF16, name="junk", tag="junk")
                nc.scalar.activation(out=junk[:], in_=fl[:, i, :], func=ACT.Copy, accum_out=ss[kind][:, i, gi:gi + 1])

        def sumsq_part(kind, gi, sqn, i):
            fp = ps_t.tile([P, 4, P], F32, name="tp", tag="tp")
            for a in range(len(sqn)):
                nc.tensor.matmul(out=fp[:, 0, :], lhsT=sqn[a][:, P * i:P * (i + 1)], rhs=ident[:], is_transpose=True,
                                 start=(a == 0), stop=(a == len(sqn) - 1))
            junk = jpool.tile([P, P], BF16, name="junk", tag="junk")
            nc.scalar.activation(out=junk[:], in_=fp[:, 0, :], func=ACT.Copy, accum_out=ss[kind][:, i, gi:gi + 1])

        def norm(kind):
            tot = const.tile([P, 4], F32, name="tot_" + kind)
            nc.vector.tensor_reduce(out=tot[:], in_=ss[kind][:, :, 0:len(SUM_GROUPS[kind])], axis=AX.X, op=ALU.add)
            nc.vector.tensor_scalar(out=tot[:], in0=tot[:], scalar1=1.0 / DI, scalar2=EPS, op0=ALU.mult, op1=ALU.add)
            rr = const.tile([P, 4], F32, name="rr_" + kind)
            nc.gpsimd.tensor_tensor(out=rr[:], in0=tot[:], in1=mhalf[:], op=ALU.pow)
            return rr

        angf = ang[:].rearrange("p c n -> p (c n)")
        ki = const.tile([P, 2 * NA], I32, name="ki")
        kf = const.tile([P, 2 * NA], F32, name="kf")
        yy = const.tile([P, 2 * NA], F32, name="yy")
        msk = const.tile([P, 2 * NA], F32, name="msk")
        sc = const.tile([P, 2, NA], F32, name="sc")
        cs = const.tile([P, 2, 4, P], F32, name="cs")
        cs5 = cs[:].rearrange("p c a (j e) -> p c a j e", e=2)

        def trig_a():
            nc.vector.tensor_scalar(out=ang[:, 1, :], in0=ang[:, 0, :], scalar1=0.5 * PI, scalar2=None, op0=ALU.add)
            nc.vector.tensor_scalar(out=ki[:], in0=angf, scalar1=1.0 / TWO_PI, scalar2=None, op0=ALU.mult)
            nc.vector.tensor_copy(out=kf[:], in_=ki[:])
            nc.vector.scalar_tensor_tensor(out=yy[:], in0=kf[:], scalar=-C1, in1=angf, op0=ALU.mult, op1=ALU.add)
            nc.vector.scalar_tensor_tensor(out=yy[:], in0=kf[:], scalar=-C2, in1=yy[:], op0=ALU.mult, op1=ALU.add)
            nc.vector.tensor_scalar(out=msk[:], in0=yy[:], scalar1=PI, scalar2=None, op0=ALU.is_gt)
            nc.vector.scalar_tensor_tensor(out=yy[:], in0=msk[:], scalar=-TWO_PI, in1=yy[:], op0=ALU.mult, op1=ALU.add)
            nc.vector.tensor_scalar(out=msk[:], in0=yy[:], scalar1=-PI, scalar2=None, op0=ALU.is_lt)
            nc.vector.scalar_tensor_tensor(out=yy[:], in0=msk[:], scalar=TWO_PI, in1=yy[:], op0=ALU.mult, op1=ALU.add)

        def trig_b():
            nc.scalar.activation(out=sc[:].rearrange("p c n -> p (c n)"), in_=yy[:], func=ACT.Sin)
            for c in range(2):
                s_ = 1 - c
                nc.gpsimd.tensor_copy(out=cs5[:, c, :, 0:22, :],
                                      in_=sc[:, s_, 0:88].rearrange("p (a j) -> p a j", a=4).unsqueeze(3).to_broadcast([P, 4, 22, 2]))
                nc.gpsimd.tensor_copy(out=cs5[:, c, :, 22:43, :],
                                      in_=sc[:, s_, 88:109].unsqueeze(1).unsqueeze(3).to_broadcast([P, 4, 21, 2]))
                nc.gpsimd.tensor_copy(out=cs5[:, c, :, 43:64, :],
                                      in_=sc[:, s_, 109:130].unsqueeze(1).unsqueeze(3).to_broadcast([P, 4, 21, 2]))
            nc.gpsimd.tensor_scalar(out=cs5[:, 1, :, :, 0], in0=cs5[:, 1, :, :, 0], scalar1=-1.0, scalar2=0.0,
                                    op0=ALU.mult, op1=ALU.add)

        trig_a()
        trig_b()
        trig_at = {}

        def rope_flips(i, u4):
            fu = ps_f.tile([P, 4, P], F32, name="fl", tag="fl")
            for a in range(4):
                nc.tensor.transpose(fu[:, a, :], u4[a][:, P * i:P * (i + 1)], ident[:])
            return fu

        def rope_unit(i, fu, rr, adder):
            if rr is None:
                m1 = upool.tile([P, S_TOK], F32, name="u", tag="u")
            else:
                m1 = mpool.tile([P, S_TOK], F32, name="m1", tag="m1")
            m2 = m2pool.tile([P, S_TOK], F32, name="m2", tag="m2")
            o1 = m1[:].rearrange("p (a n) -> p a n", a=4)
            c1 = cs[:, 0, i, :].unsqueeze(1).to_broadcast([P, 4, P])
            o2 = m2[:].rearrange("p (a j e) -> p a j e", a=4, e=2)
            f2 = fu[:].rearrange("p a (j e) -> p a j e", e=2)[:, :, :, ::-1]
            c2 = cs[:, 1, i, :].rearrange("p (j e) -> p j e", e=2).unsqueeze(1).to_broadcast([P, 4, 64, 2])
            if rr is None:
                nc.vector.tensor_tensor(out=o1, in0=fu[:], in1=c1, op=ALU.mult)
                nc.vector.tensor_tensor(out=o2, in0=f2, in1=c2, op=ALU.mult)
            else:
                nc.vector.scalar_tensor_tensor(out=o1, in0=fu[:], scalar=rr[:, i:i + 1], in1=c1, op0=ALU.mult, op1=ALU.mult)
                nc.vector.scalar_tensor_tensor(out=o2, in0=f2, scalar=rr[:, i:i + 1], in1=c2, op0=ALU.mult, op1=ALU.mult)
            adder.tensor_tensor(out=m1[:], in0=m1[:], in1=m2[:], op=ALU.add)
            return m1

        def store(queue, kind, i, gi, m1):
            queue.dma_start(out=outs[kind][P * i:P * (i + 1), 512 * gi:512 * (gi + 1)], in_=m1[:])

        ctx.enter_context(tc.manual_schedule())
        heads = [("k", j) for j in range(NH)] + [("q", j) for j in range(NH)]
        N = len(heads)
        prod_at = {}
        for j in range(NH):
            st = j + 2 if j < NPRE else max(17 + j - NPRE, j + 2)
            prod_at.setdefault(st, []).append(j)
            if j > 0:
                prod_at.setdefault(("load", max(st - 2, 0)), []).append(j)
        gws = {}
        cds = {}
        us = {"q": [], "k": []}
        sqs = {"q": [], "k": []}
        rrs = {}
        parts = {}
        ready = []
        taken = 0
        early = []
        for s in range(N + 4):
            n_units = 0 if s < 19 else (1 if s < 23 or s % 2 == 0 else 2)
            todo = ready[taken:taken + n_units]
            taken += len(todo)
            fus = [rope_flips(i, us[kind][4 * gi:4 * gi + 4]) for kind, i, gi in todo]
            if s + 2 < NH:
                src[s + 2] = load_rows(Wk[P * (s + 2):P * (s + 3), :])
            for j in prod_at.get(("load", s), []):
                q8[j] = load_q8(j)
            if s < N:
                gws[s] = flip_head(src[s])
            if 0 <= s - 1 < N:
                cds[s - 1] = quant_head(gws[s - 1])
            for j in prod_at.get(s, []):
                src[NH + j] = product(q8[j])
            if 0 <= s - 3 < N:
                kind, j = heads[s - 3]
                u, sq = mx_head(cds[s - 3][0], cds[s - 3][1], j if kind == "q" else NH + j)
                us[kind].append(u)
                sqs[kind].append(sq)
                if kind == "q" and j % 4 == 3 and j // 4 < IMM:
                    ready.extend([("q", i, j // 4) for i in range(4)])
            for (kind, i, gi), fu in zip(todo, fus):
                if kind == "k":
                    store(nc.sync, "k", i, gi, rope_unit(i, fu, rrs["k"], nc.gpsimd))
                else:
                    early.append((i, gi, rope_unit(i, fu, None, nc.gpsimd)))
            if s in trig_at:
                trig_at[s]()
            if s - 4 >= 0:
                kind, j = heads[s - 4]
                for gi, hs in enumerate(SUM_GROUPS[kind]):
                    if hs[-1] == j and gi < 3:
                        for i in range(4):
                            parts.setdefault(s + i, []).append((kind, gi, hs, i))
                    elif hs[-1] == j:
                        sumsq(kind, gi, [sqs[kind][h] for h in hs])
                for pk, gi, hs, i in parts.get(s, []):
                    sumsq_part(pk, gi, [sqs[pk][h] for h in hs], i)
                if j == NH - 1:
                    rrs[kind] = norm(kind)
                    if kind == "k":
                        ready.extend([("k", i, gi) for gi in range(4) for i in range(4)])

        for kind, i, gi in ready[taken:]:
            fu = rope_flips(i, us[kind][4 * gi:4 * gi + 4])
            if kind == "k":
                store(nc.sync, "k", i, gi, rope_unit(i, fu, rrs["k"], nc.gpsimd))
            else:
                early.append((i, gi, rope_unit(i, fu, None, nc.gpsimd)))
        for i, gi, m1 in early:
            nc.scalar.activation(out=m1[:], in_=m1[:], func=ACT.Copy, scale=rrs["q"][:, i:i + 1])
            store(nc.scalar, "q", i, gi, m1)
        for gi in range(IMM, 4):
            for i in range(4):
                last = (gi == 3 and i == 3)
                store(nc.sync, "q", i, gi, rope_unit(i, rope_flips(i, us["q"][4 * gi:4 * gi + 4]), rrs["q"], nc.vector if last else nc.gpsimd))
